import numpy as np
import ml_dtypes


def mxq(x, axis, fmt="e4m3"):
    dtype, down = {"e4m3": (ml_dtypes.float8_e4m3fn, 7), "e5m2": (ml_dtypes.float8_e5m2, 14)}[fmt]
    v = np.moveaxis(np.asarray(x, np.float32).astype(ml_dtypes.bfloat16).astype(np.float64), axis, -1)
    blocks = v.reshape(v.shape[:-1] + (-1, 32))
    amax = np.abs(blocks).max(-1, keepdims=True)
    byte = np.maximum(np.where(amax > 0, np.frexp(amax)[1] - 1 + 127, 0) - down, 1)
    scale = np.exp2(byte - 127.0)
    codes = (blocks / scale).astype(np.float32).astype(dtype).astype(np.float64)
    return np.moveaxis((codes * scale).reshape(v.shape), -1, axis)


WIDE = False


def mx_kscale(k):
    if not WIDE:
        return np.ones(k)
    levels = np.array([10, -10, 5, -5, 0])
    if k % 512:
        return np.exp2(np.random.permutation(np.resize(levels, k // 32))).repeat(32)
    a = np.empty((k // 512, 16))
    for p in range(k // 512):
        a[p, :8] = np.random.permutation(np.resize(levels, 8))
        for g in range(8):
            far = levels[np.abs(levels - a[p, g]) >= 10]
            a[p, g + 8] = far[np.random.randint(len(far))]
    return np.exp2(a.ravel()).repeat(32)


BF16 = ml_dtypes.bfloat16


def bf(x):
    return np.asarray(x, np.float32).astype(BF16)


def f64(x):
    return np.asarray(x).astype(np.float64)


E2M1 = np.array([0.0, 0.5, 1.0, 1.5, 2.0, 3.0, 4.0, 6.0, -0.0, -0.5, -1.0, -1.5, -2.0, -3.0, -4.0, -6.0])


def pack_weight(w, fmt):
    k, n = w.shape
    w = f64(bf(w)).reshape(k // 32, 32, n)
    amax = np.abs(w).max(1)
    if fmt == "e4m3":
        byte = np.frexp(amax)[1] - 1 + 127 - 7
    else:
        mant, ex = np.frexp(amax / 6.0)
        byte = np.where(mant > 0.5, ex, ex - 1) + 127
    byte = np.clip(np.where(amax > 0, byte, 1), 1, 254)
    scaled = (w * np.exp2(127.0 - byte)[:, None, :]).reshape(k, n).astype(np.float32)
    by_word = np.ascontiguousarray(scaled.reshape(k // 512, 128, 4, n).transpose(0, 1, 3, 2))
    if fmt == "e4m3":
        words = by_word.astype(ml_dtypes.float8_e4m3fn).view(np.uint8)
    else:
        c = by_word.astype(ml_dtypes.float4_e2m1fn).view(np.uint8) & 0xF
        words = c[..., 0::2] | (c[..., 1::2] << 4)
    return np.ascontiguousarray(words), np.ascontiguousarray(byte.astype(np.uint8).reshape(k // 512, 16, n))


def unpack_weight(words, scales, fmt):
    g, p, n, _ = words.shape
    if fmt == "e4m3":
        vals = np.ascontiguousarray(words).view(ml_dtypes.float8_e4m3fn).astype(np.float64)
    else:
        nib = np.empty((g, p, n, 4), np.uint8)
        nib[..., 0::2] = words & 0xF
        nib[..., 1::2] = words >> 4
        vals = E2M1[nib]
    vals = vals * np.repeat(np.exp2(scales.astype(np.float64) - 127.0), 8, axis=1)[..., None]
    return vals.transpose(0, 1, 3, 2).reshape(g * 512, n)


B, H, W, C, I, O, NH = 1, 2, 256, 8192, 512, 512, 8
DH = I // NH
SCALE = DH ** -0.5
FMT = "e4m3"


def setup_inputs():
    s, t = mx_kscale(C), mx_kscale(I)
    sc = s[None, :, None, None]
    left_feat = bf(np.random.standard_normal((B, C, H, W)) * sc)
    right_feat = bf(np.random.standard_normal((B, C, H, W)) * sc)
    wq = np.random.standard_normal((I, C)) / np.sqrt(C) / s[None, :] * t[:, None]
    wk = np.random.standard_normal((I, C)) / np.sqrt(C) / s[None, :] / t[:, None]
    wq_words, wq_scales = pack_weight(np.ascontiguousarray(wq.T), FMT)
    wk_words, wk_scales = pack_weight(np.ascontiguousarray(wk.T), FMT)
    return {"left_feat": left_feat,
            "right_feat": right_feat,
            "wq_words": wq_words, "wq_scales": wq_scales,
            "wk_words": wk_words, "wk_scales": wk_scales}


def reference(left_feat, right_feat, wq_words, wq_scales, wk_words, wk_scales):
    lf = f64(left_feat).reshape(B, C, H * W)
    rf = f64(right_feat).reshape(B, C, H * W)
    q = unpack_weight(wq_words, wq_scales, FMT).T @ mxq(lf, 1, "e4m3")
    k = unpack_weight(wk_words, wk_scales, FMT).T @ mxq(rf, 1, "e4m3")
    q = q.reshape(B, I, H, W).transpose(0, 2, 3, 1)
    k = k.reshape(B, I, H, W).transpose(0, 2, 1, 3)
    return (mxq(q, 3, "e4m3") @ mxq(k, 2, "e4m3")) * SCALE

@@ -1,0 +1,216 @@
+import concourse.mybir as mybir
+from concourse.masks import make_identity
+
+FP8X4 = mybir.dt.float8_e4m3fn_x4
+BF16 = mybir.dt.bfloat16
+F32 = mybir.dt.float32
+I32 = mybir.dt.int32
+U32 = mybir.dt.uint32
+U8 = mybir.dt.uint8
+COPY = mybir.ActivationFunctionType.Copy
+
+P = 128
+PACK = 4
+PAIRS = 2
+K_PASS = P * PACK
+C = 8192
+PASSES = C // K_PASS
+H = 2
+W = 256
+HW = H * W
+O = 512
+HW_TILES = HW // P
+W_TILES = W // P
+QUADRANTS = 4
+SHARED = 4
+LEAD = 2
+RUN = 4
+SCALE = 0.125
+
+FLOPS = 2 * 2 * O * C * HW + 2 * H * W * W * O
+
+
+def tile_sttm_single_pa_k_kernel(
+    tc, left_feat, right_feat, wq_words, wq_scales, wk_words, wk_scales, out
+):
+    nc = tc.nc
+    sides = ("q", "k")
+    feature = {
+        "q": left_feat[0].rearrange("(g p t) h w -> p g t (h w)", p=P, t=PACK),
+        "k": right_feat[0].rearrange("(g p t) h w -> p g t (h w)", p=P, t=PACK),
+    }
+    words = {
+        "q": wq_words.rearrange("g p n t -> p g (n t)").bitcast(I32),
+        "k": wk_words.rearrange("g p n t -> p g (n t)").bitcast(I32),
+    }
+    scale_rows = {"q": wq_scales.bitcast(I32), "k": wk_scales.bitcast(I32)}
+    steps = [(side, g) for side in sides for g in range(PASSES)]
+
+    with (
+        tc.tile_pool(name="keep", bufs=1) as keep,
+        tc.tile_pool(name="raw", bufs=8) as raw_pool,
+        tc.tile_pool(name="stage", bufs=4) as stage,
+        tc.tile_pool(name="quantised", bufs=6) as quantised,
+        tc.psum_pool(name="psum", bufs=1) as psum,
+        tc.manual_schedule(),
+    ):
+        identity = keep.tile([P, P], F32, name="identity")
+        make_identity(nc, identity[:])
+        w_codes = {}
+        w_planes = {}
+        codes = {}
+        planes = {}
+        for side in sides:
+            w_codes[side] = keep.tile([P, PASSES, O], U32, name="w_codes_" + side, align_bytes=64)
+            w_planes[side] = keep.tile(
+                [P, PASSES // SHARED, O], U8, name="w_planes_" + side, align_bytes=64
+            )
+            codes[side] = keep.tile([P, HW], U32, name="codes_" + side, align_bytes=64)
+            planes[side] = keep.tile([P, HW], U8, name="planes_" + side, align_bytes=64)
+            nc.vector.memset(w_planes[side][:].bitcast(I32), 0)
+
+        def load_feature(step):
+            side, g = steps[step]
+            raw = raw_pool.tile([P, PACK, HW], BF16, name="raw")
+            nc.sync.dma_start(out=raw[:], in_=feature[side][:, g])
+            return raw
+
+        def load_scale_planes(side, block):
+            passes = slice(SHARED * block, SHARED * (block + 1))
+            for quadrant in range(QUADRANTS):
+                nc.sync.dma_start(
+                    out=w_planes[side][32 * quadrant : 32 * quadrant + 16, block, :].bitcast(I32),
+                    in_=scale_rows[side][passes, 4 * quadrant : 4 * quadrant + 4, :],
+                )
+
+        def regroup_feature(raw):
+            grouped = stage.tile([P, HW, PACK], BF16, name="grouped", align_bytes=64)
+            for h, copy in enumerate((nc.vector.tensor_copy, nc.scalar.copy)):
+                cols = slice(h * W, (h + 1) * W)
+                copy(
+                    out=grouped[:, cols, :].rearrange("p (c i) t -> p c t i", i=RUN),
+                    in_=raw[:, :, cols].rearrange("p t (c i) -> p c t i", i=RUN),
+                )
+            return grouped
+
+        def round_product(acc):
+            rounded = []
+            for i in range(HW_TILES):
+                tile = stage.tile([P, O], BF16, name="rounded")
+                copy = nc.vector.tensor_copy if i % 2 == 0 else nc.scalar.copy
+                copy(out=tile[:], in_=acc[i][:])
+                rounded.append(tile)
+            return rounded
+
+        def turn_product(rounded):
+            turned = []
+            for i in range(HW_TILES):
+                tile = psum.tile([P, PAIRS, P], F32, name="turned%d" % i, tag="bank%d" % i)
+                pair_words = rounded[i][:].bitcast(F32)
+                for u in range(PAIRS):
+                    nc.tensor.transpose(tile[:, u, :], pair_words[:, u::PAIRS], identity[:])
+                turned.append(tile)
+            return turned
+
+        def regroup_product(turned):
+            grouped = []
+            for h in range(H):
+                tile = stage.tile([P, W, PACK], BF16, name="product", align_bytes=64)
+                for i in range(W_TILES):
+                    copy = nc.vector.tensor_copy if h == 0 and i == 0 else nc.scalar.copy
+                    copy(
+                        out=tile[:, i * P : (i + 1) * P, :].rearrange("p x t -> p (x t)").bitcast(F32),
+                        in_=turned[h * W_TILES + i][:].rearrange("p u x -> p x u"),
+                    )
+                grouped.append(tile)
+            return grouped
+
+        def quantise_product(side, grouped):
+            for h in range(H):
+                cols = slice(h * W, (h + 1) * W)
+                nc.vector.quantize_mx(
+                    out=codes[side][:, cols].bitcast(FP8X4),
+                    scales=planes[side][:, cols],
+                    in_=grouped[h][:].rearrange("p x t -> p (x t)"),
+                )
+
+        raws = {}
+        for step in range(LEAD):
+            raws[step] = load_feature(step)
+        groupeds = {0: regroup_feature(raws[0])}
+
+        acc = {}
+        for step, (side, g) in enumerate(steps):
+            if step + LEAD < len(steps):
+                raws[step + LEAD] = load_feature(step + LEAD)
+            if g % SHARED == 0:
+                load_scale_planes(side, g // SHARED)
+            nc.sync.dma_start(out=w_codes[side][:, g, :].bitcast(I32), in_=words[side][:, g, :])
+
+            if step + 1 < len(steps):
+                groupeds[step + 1] = regroup_feature(raws[step + 1])
+            f_codes = quantised.tile([P, HW], U32, name="f_codes", align_bytes=64)
+            f_planes = quantised.tile([P, HW], U8, name="f_planes", align_bytes=64)
+            nc.vector.quantize_mx(
+                out=f_codes[:].bitcast(FP8X4),
+                scales=f_planes[:],
+                in_=groupeds[step][:].rearrange("p x t -> p (x t)"),
+            )
+
+            if g == 0:
+                first = HW_TILES * sides.index(side)
+                acc[side] = [
+                    psum.tile([P, O], F32, name="acc%d" % (first + i), tag="bank%d" % (first + i))
+                    for i in range(HW_TILES)
+                ]
+            block, j = divmod(g, SHARED)
+            for i in range(HW_TILES):
+                positions = slice(i * P, (i + 1) * P)
+                nc.tensor.matmul_mx(
+                    out=acc[side][i][:],
+                    lhsT=f_codes[:, positions].bitcast(FP8X4),
+                    lhsT_scale=f_planes[:, positions],
+                    rhs=w_codes[side][:, g, :].bitcast(FP8X4),
+                    rhs_scale=w_planes[side][4 * j : P, block, :],
+                    start=(g == 0),
+                    stop=(g == PASSES - 1),
+                )
+
+            if side == "k":
+                if g == 0:
+                    q_rounded = round_product(acc["q"])
+                elif g == 1:
+                    q_turned = turn_product(q_rounded)
+                elif g == 2:
+                    q_grouped = regroup_product(q_turned)
+                elif g == 3:
+                    quantise_product("q", q_grouped)
+
+        k_rounded = round_product(acc["k"])
+        k_turned = turn_product(k_rounded)
+        k_grouped = regroup_product(k_turned)
+        quantise_product("k", k_grouped)
+
+        for h in range(H):
+            x_cols = slice(h * W, (h + 1) * W)
+            for i in range(W_TILES):
+                tile_index = h * W_TILES + i
+                w_cols = slice(tile_index * P, (tile_index + 1) * P)
+                dots = psum.tile(
+                    [P, W], F32, name="dots%d" % tile_index, tag="bank%d" % (HW_TILES + tile_index)
+                )
+                nc.tensor.matmul_mx(
+                    out=dots[:],
+                    lhsT=codes["q"][:, w_cols].bitcast(FP8X4),
+                    lhsT_scale=planes["q"][:, w_cols],
+                    rhs=codes["k"][:, x_cols].bitcast(FP8X4),
+                    rhs_scale=planes["k"][:, x_cols],
+                    start=True,
+                    stop=True,
+                )
+                result = stage.tile([P, W], F32, name="result")
+                if i == 0:
+                    nc.vector.tensor_scalar_mul(out=result[:], in0=dots[:], scalar1=SCALE)
+                else:
+                    nc.scalar.activation(out=result[:], in_=dots[:], func=COPY, scale=SCALE)
+                nc.sync.dma_start(out=out[0, h, i * P : (i + 1) * P, :], in_=result[:])

@@ -23,7 +23,9 @@ HW_TILES = HW // P
 W_TILES = W // P
 QUADRANTS = 4
 SHARED = 4
-LEAD = 2
+AT_ONCE = 3
+FINE = 2
+SHARES = (320, 192)
 RUN = 4
 SCALE = 0.125
 
@@ -69,10 +71,13 @@ def tile_sttm_single_pa_k_kernel(
             planes[side] = keep.tile([P, HW], U8, name="planes_" + side, align_bytes=64)
             nc.vector.memset(w_planes[side][:].bitcast(I32), 0)
 
-        def load_feature(step):
+        def load_step(step):
             side, g = steps[step]
             raw = raw_pool.tile([P, PACK, HW], BF16, name="raw")
             nc.sync.dma_start(out=raw[:], in_=feature[side][:, g])
+            if g % SHARED == 0:
+                load_scale_planes(side, g // SHARED)
+            nc.sync.dma_start(out=w_codes[side][:, g, :].bitcast(I32), in_=words[side][:, g, :])
             return raw
 
         def load_scale_planes(side, block):
@@ -83,21 +88,36 @@ def tile_sttm_single_pa_k_kernel(
                     in_=scale_rows[side][passes, 4 * quadrant : 4 * quadrant + 4, :],
                 )
 
-        def regroup_feature(raw):
+        def regroup_feature(raw, widths):
             grouped = stage.tile([P, HW, PACK], BF16, name="grouped", align_bytes=64)
-            for h, copy in enumerate((nc.vector.tensor_copy, nc.scalar.copy)):
-                cols = slice(h * W, (h + 1) * W)
+            start = 0
+            for piece, width in enumerate(widths):
+                copy = nc.vector.tensor_copy if piece % 2 == 0 else nc.scalar.copy
+                cols = slice(start, start + width)
+                start += width
                 copy(
                     out=grouped[:, cols, :].rearrange("p (c i) t -> p c t i", i=RUN),
                     in_=raw[:, :, cols].rearrange("p t (c i) -> p c t i", i=RUN),
                 )
             return grouped
 
+        def quantise_feature(grouped, width):
+            f_codes = quantised.tile([P, HW], U32, name="f_codes", align_bytes=64)
+            f_planes = quantised.tile([P, HW], U8, name="f_planes", align_bytes=64)
+            for piece in range(HW // width):
+                cols = slice(piece * width, (piece + 1) * width)
+                nc.vector.quantize_mx(
+                    out=f_codes[:, cols].bitcast(FP8X4),
+                    scales=f_planes[:, cols],
+                    in_=grouped[:, cols, :].rearrange("p x t -> p (x t)"),
+                )
+            return f_codes, f_planes
+
         def round_product(acc):
             rounded = []
             for i in range(HW_TILES):
                 tile = stage.tile([P, O], BF16, name="rounded")
-                copy = nc.vector.tensor_copy if i % 2 == 0 else nc.scalar.copy
+                copy = nc.scalar.copy if i % 2 == 0 else nc.vector.tensor_copy
                 copy(out=tile[:], in_=acc[i][:])
                 rounded.append(tile)
             return rounded
@@ -117,7 +137,7 @@ def tile_sttm_single_pa_k_kernel(
             for h in range(H):
                 tile = stage.tile([P, W, PACK], BF16, name="product", align_bytes=64)
                 for i in range(W_TILES):
-                    copy = nc.vector.tensor_copy if h == 0 and i == 0 else nc.scalar.copy
+                    copy = nc.vector.tensor_copy if h == 0 and i == 1 else nc.scalar.copy
                     copy(
                         out=tile[:, i * P : (i + 1) * P, :].rearrange("p x t -> p (x t)").bitcast(F32),
                         in_=turned[h * W_TILES + i][:].rearrange("p u x -> p x u"),
@@ -134,28 +154,20 @@ def tile_sttm_single_pa_k_kernel(
                     in_=grouped[h][:].rearrange("p x t -> p (x t)"),
                 )
 
-        raws = {}
-        for step in range(LEAD):
-            raws[step] = load_feature(step)
-        groupeds = {0: regroup_feature(raws[0])}
+        last = len(steps) - 1
+        raws = {0: load_step(0)}
+        groupeds = {0: regroup_feature(raws[0], SHARES)}
 
         acc = {}
         for step, (side, g) in enumerate(steps):
-            if step + LEAD < len(steps):
-                raws[step + LEAD] = load_feature(step + LEAD)
-            if g % SHARED == 0:
-                load_scale_planes(side, g // SHARED)
-            nc.sync.dma_start(out=w_codes[side][:, g, :].bitcast(I32), in_=words[side][:, g, :])
-
-            if step + 1 < len(steps):
-                groupeds[step + 1] = regroup_feature(raws[step + 1])
-            f_codes = quantised.tile([P, HW], U32, name="f_codes", align_bytes=64)
-            f_planes = quantised.tile([P, HW], U8, name="f_planes", align_bytes=64)
-            nc.vector.quantize_mx(
-                out=f_codes[:].bitcast(FP8X4),
-                scales=f_planes[:],
-                in_=groupeds[step][:].rearrange("p x t -> p (x t)"),
-            )
+            if step < last:
+                raws[step + 1] = load_step(step + 1)
+            if step + 1 <= last - AT_ONCE:
+                groupeds[step + 1] = regroup_feature(raws[step + 1], SHARES)
+            fine = step > last - FINE
+            if step > last - AT_ONCE:
+                groupeds[step] = regroup_feature(raws[step], [P] * HW_TILES if fine else SHARES)
+            f_codes, f_planes = quantise_feature(groupeds[step], P if fine else HW)
 
             if g == 0:
                 first = HW_TILES * sides.index(side)

@@ -26,6 +26,7 @@ SHARED = 4
 AT_ONCE = 3
 FINE = 2
 SHARES = (320, 192)
+BATCHES = {"q": (1, 1) + (2,) * 7, "k": (2,) * 6 + (1,) * 4}
 RUN = 4
 SCALE = 0.125
 
@@ -50,7 +51,7 @@ def tile_sttm_single_pa_k_kernel(
 
     with (
         tc.tile_pool(name="keep", bufs=1) as keep,
-        tc.tile_pool(name="raw", bufs=8) as raw_pool,
+        tc.tile_pool(name="raw", bufs=6) as raw_pool,
         tc.tile_pool(name="stage", bufs=4) as stage,
         tc.tile_pool(name="quantised", bufs=6) as quantised,
         tc.psum_pool(name="psum", bufs=1) as psum,
@@ -71,14 +72,14 @@ def tile_sttm_single_pa_k_kernel(
             planes[side] = keep.tile([P, HW], U8, name="planes_" + side, align_bytes=64)
             nc.vector.memset(w_planes[side][:].bitcast(I32), 0)
 
-        def load_step(step):
-            side, g = steps[step]
-            raw = raw_pool.tile([P, PACK, HW], BF16, name="raw")
-            nc.sync.dma_start(out=raw[:], in_=feature[side][:, g])
+        def load_batch(side, g, count):
+            passes = slice(g, g + count)
+            raw = raw_pool.tile([P, count, PACK, HW], BF16, name="raw")
+            nc.sync.dma_start(out=raw[:], in_=feature[side][:, passes])
             if g % SHARED == 0:
                 load_scale_planes(side, g // SHARED)
-            nc.sync.dma_start(out=w_codes[side][:, g, :].bitcast(I32), in_=words[side][:, g, :])
-            return raw
+            nc.sync.dma_start(out=w_codes[side][:, passes, :].bitcast(I32), in_=words[side][:, passes, :])
+            return [raw[:, i] for i in range(count)]
 
         def load_scale_planes(side, block):
             passes = slice(SHARED * block, SHARED * (block + 1))
@@ -134,34 +135,39 @@ def tile_sttm_single_pa_k_kernel(
 
         def regroup_product(turned):
             grouped = []
-            for h in range(H):
-                tile = stage.tile([P, W, PACK], BF16, name="product", align_bytes=64)
-                for i in range(W_TILES):
-                    copy = nc.vector.tensor_copy if h == 0 and i == 1 else nc.scalar.copy
-                    copy(
-                        out=tile[:, i * P : (i + 1) * P, :].rearrange("p x t -> p (x t)").bitcast(F32),
-                        in_=turned[h * W_TILES + i][:].rearrange("p u x -> p x u"),
-                    )
+            for i in range(HW_TILES):
+                tile = stage.tile([P, P, PACK], BF16, name="product", align_bytes=64)
+                copy = nc.vector.tensor_copy if i == 1 else nc.scalar.copy
+                copy(
+                    out=tile[:].rearrange("p x t -> p (x t)").bitcast(F32),
+                    in_=turned[i][:].rearrange("p u x -> p x u"),
+                )
                 grouped.append(tile)
             return grouped
 
         def quantise_product(side, grouped):
-            for h in range(H):
-                cols = slice(h * W, (h + 1) * W)
+            for i in range(HW_TILES):
+                cols = slice(i * P, (i + 1) * P)
                 nc.vector.quantize_mx(
                     out=codes[side][:, cols].bitcast(FP8X4),
                     scales=planes[side][:, cols],
-                    in_=grouped[h][:].rearrange("p x t -> p (x t)"),
+                    in_=grouped[i][:].rearrange("p x t -> p (x t)"),
                 )
 
         last = len(steps) - 1
-        raws = {0: load_step(0)}
+        batch_at = {}
+        for number, side in enumerate(sides):
+            g = 0
+            for count in BATCHES[side]:
+                batch_at[number * PASSES + g] = (side, g, count)
+                g += count
+        raws = load_batch(*batch_at[0])
         groupeds = {0: regroup_feature(raws[0], SHARES)}
 
         acc = {}
         for step, (side, g) in enumerate(steps):
-            if step < last:
-                raws[step + 1] = load_step(step + 1)
+            if step + 1 in batch_at:
+                raws += load_batch(*batch_at[step + 1])
             if step + 1 <= last - AT_ONCE:
                 groupeds[step + 1] = regroup_feature(raws[step + 1], SHARES)
             fine = step > last - FINE
@@ -203,16 +209,15 @@ def tile_sttm_single_pa_k_kernel(
         k_grouped = regroup_product(k_turned)
         quantise_product("k", k_grouped)
 
-        for h in range(H):
-            x_cols = slice(h * W, (h + 1) * W)
-            for i in range(W_TILES):
-                tile_index = h * W_TILES + i
-                w_cols = slice(tile_index * P, (tile_index + 1) * P)
-                dots = psum.tile(
-                    [P, W], F32, name="dots%d" % tile_index, tag="bank%d" % (HW_TILES + tile_index)
-                )
+        for i in range(HW_TILES):
+            h, x_tile = divmod(i, W_TILES)
+            x_cols = slice(i * P, (i + 1) * P)
+            bank = "bank%d" % (HW_TILES + i)
+            dots = psum.tile([P, W_TILES, P], F32, name="dots%d" % i, tag=bank)
+            for w_tile in range(W_TILES):
+                w_cols = slice(h * W + w_tile * P, h * W + (w_tile + 1) * P)
                 nc.tensor.matmul_mx(
-                    out=dots[:],
+                    out=dots[:, w_tile, :],
                     lhsT=codes["q"][:, w_cols].bitcast(FP8X4),
                     lhsT_scale=planes["q"][:, w_cols],
                     rhs=codes["k"][:, x_cols].bitcast(FP8X4),
@@ -220,9 +225,12 @@ def tile_sttm_single_pa_k_kernel(
                     start=True,
                     stop=True,
                 )
-                result = stage.tile([P, W], F32, name="result")
-                if i == 0:
-                    nc.vector.tensor_scalar_mul(out=result[:], in0=dots[:], scalar1=SCALE)
-                else:
-                    nc.scalar.activation(out=result[:], in_=dots[:], func=COPY, scale=SCALE)
-                nc.sync.dma_start(out=out[0, h, i * P : (i + 1) * P, :], in_=result[:])
+            result = stage.tile([P, W_TILES, P], F32, name="result")
+            if i % 2 == 0:
+                nc.scalar.activation(out=result[:], in_=dots[:], func=COPY, scale=SCALE)
+            else:
+                nc.vector.tensor_scalar_mul(out=result[:], in0=dots[:], scalar1=SCALE)
+            nc.sync.dma_start(
+                out=out[0, h].rearrange("(i p) x -> p i x", p=P)[:, :, x_tile * P : (x_tile + 1) * P],
+                in_=result[:],
+            )

@@ -25,8 +25,9 @@ QUADRANTS = 4
 SHARED = 4
 AT_ONCE = 3
 FINE = 2
-SHARES = (320, 192)
-BATCHES = {"q": (1, 1) + (2,) * 7, "k": (2,) * 6 + (1,) * 4}
+SHARES = (288, 224)
+SHARES_AT_ONCE = (320, 192)
+BATCHES = {"q": (1, 1) + (2,) * 7, "k": (2,) * 5 + (1,) * 6}
 RUN = 4
 SCALE = 0.125
 
@@ -172,7 +173,7 @@ def tile_sttm_single_pa_k_kernel(
                 groupeds[step + 1] = regroup_feature(raws[step + 1], SHARES)
             fine = step > last - FINE
             if step > last - AT_ONCE:
-                groupeds[step] = regroup_feature(raws[step], [P] * HW_TILES if fine else SHARES)
+                groupeds[step] = regroup_feature(raws[step], [P] * HW_TILES if fine else SHARES_AT_ONCE)
             f_codes, f_planes = quantise_feature(groupeds[step], P if fine else HW)
 
             if g == 0:

@@ -23,8 +23,8 @@ HW_TILES = HW // P
 W_TILES = W // P
 QUADRANTS = 4
 SHARED = 4
-AT_ONCE = 3
-FINE = 2
+AT_ONCE = 4
+FINE = 3
 SHARES = (288, 224)
 SHARES_AT_ONCE = (320, 192)
 BATCHES = {"q": (1, 1) + (2,) * 7, "k": (2,) * 5 + (1,) * 6}
@@ -120,7 +120,10 @@ def tile_sttm_single_pa_k_kernel(
             for i in range(HW_TILES):
                 tile = stage.tile([P, O], BF16, name="rounded")
                 copy = nc.scalar.copy if i % 2 == 0 else nc.vector.tensor_copy
-                copy(out=tile[:], in_=acc[i][:])
+                copy(
+                    out=tile[:].rearrange("x (u p e) -> x u p e", u=PAIRS, e=PACK // PAIRS),
+                    in_=acc[i][:].rearrange("x (p u e) -> x u p e", u=PAIRS, e=PACK // PAIRS),
+                )
                 rounded.append(tile)
             return rounded
 
@@ -130,7 +133,7 @@ def tile_sttm_single_pa_k_kernel(
                 tile = psum.tile([P, PAIRS, P], F32, name="turned%d" % i, tag="bank%d" % i)
                 pair_words = rounded[i][:].bitcast(F32)
                 for u in range(PAIRS):
-                    nc.tensor.transpose(tile[:, u, :], pair_words[:, u::PAIRS], identity[:])
+                    nc.tensor.transpose(tile[:, u, :], pair_words[:, u * P : (u + 1) * P], identity[:])
                 turned.append(tile)
             return turned
 

import concourse.mybir as mybir
from concourse.masks import make_identity

FP8X4 = mybir.dt.float8_e4m3fn_x4
BF16 = mybir.dt.bfloat16
F32 = mybir.dt.float32
I32 = mybir.dt.int32
U32 = mybir.dt.uint32
U8 = mybir.dt.uint8
COPY = mybir.ActivationFunctionType.Copy

P = 128
PACK = 4
PAIRS = 2
K_PASS = P * PACK
C = 8192
PASSES = C // K_PASS
H = 2
W = 256
HW = H * W
O = 512
HW_TILES = HW // P
W_TILES = W // P
QUADRANTS = 4
SHARED = 4
AT_ONCE = 4
FINE = 3
SHARES = (288, 224)
SHARES_AT_ONCE = (320, 192)
BATCHES = {"q": (1, 1) + (2,) * 7, "k": (2,) * 5 + (1,) * 6}
RUN = 4
SCALE = 0.125

FLOPS = 2 * 2 * O * C * HW + 2 * H * W * W * O


def tile_sttm_single_pa_k_kernel(
    tc, left_feat, right_feat, wq_words, wq_scales, wk_words, wk_scales, out
):
    nc = tc.nc
    sides = ("q", "k")
    feature = {
        "q": left_feat[0].rearrange("(g p t) h w -> p g t (h w)", p=P, t=PACK),
        "k": right_feat[0].rearrange("(g p t) h w -> p g t (h w)", p=P, t=PACK),
    }
    words = {
        "q": wq_words.rearrange("g p n t -> p g (n t)").bitcast(I32),
        "k": wk_words.rearrange("g p n t -> p g (n t)").bitcast(I32),
    }
    scale_rows = {"q": wq_scales.bitcast(I32), "k": wk_scales.bitcast(I32)}
    steps = [(side, g) for side in sides for g in range(PASSES)]

    with (
        tc.tile_pool(name="keep", bufs=1) as keep,
        tc.tile_pool(name="raw", bufs=6) as raw_pool,
        tc.tile_pool(name="stage", bufs=4) as stage,
        tc.tile_pool(name="quantised", bufs=6) as quantised,
        tc.psum_pool(name="psum", bufs=1) as psum,
        tc.manual_schedule(),
    ):
        identity = keep.tile([P, P], F32, name="identity")
        make_identity(nc, identity[:])
        w_codes = {}
        w_planes = {}
        codes = {}
        planes = {}
        for side in sides:
            w_codes[side] = keep.tile([P, PASSES, O], U32, name="w_codes_" + side, align_bytes=64)
            w_planes[side] = keep.tile(
                [P, PASSES // SHARED, O], U8, name="w_planes_" + side, align_bytes=64
            )
            codes[side] = keep.tile([P, HW], U32, name="codes_" + side, align_bytes=64)
            planes[side] = keep.tile([P, HW], U8, name="planes_" + side, align_bytes=64)
            nc.vector.memset(w_planes[side][:].bitcast(I32), 0)

        def load_batch(side, g, count):
            passes = slice(g, g + count)
            raw = raw_pool.tile([P, count, PACK, HW], BF16, name="raw")
            nc.sync.dma_start(out=raw[:], in_=feature[side][:, passes])
            if g % SHARED == 0:
                load_scale_planes(side, g // SHARED)
            nc.sync.dma_start(out=w_codes[side][:, passes, :].bitcast(I32), in_=words[side][:, passes, :])
            return [raw[:, i] for i in range(count)]

        def load_scale_planes(side, block):
            passes = slice(SHARED * block, SHARED * (block + 1))
            for quadrant in range(QUADRANTS):
                nc.sync.dma_start(
                    out=w_planes[side][32 * quadrant : 32 * quadrant + 16, block, :].bitcast(I32),
                    in_=scale_rows[side][passes, 4 * quadrant : 4 * quadrant + 4, :],
                )

        def regroup_feature(raw, widths):
            grouped = stage.tile([P, HW, PACK], BF16, name="grouped", align_bytes=64)
            start = 0
            for piece, width in enumerate(widths):
                copy = nc.vector.tensor_copy if piece % 2 == 0 else nc.scalar.copy
                cols = slice(start, start + width)
                start += width
                copy(
                    out=grouped[:, cols, :].rearrange("p (c i) t -> p c t i", i=RUN),
                    in_=raw[:, :, cols].rearrange("p t (c i) -> p c t i", i=RUN),
                )
            return grouped

        def quantise_feature(grouped, width):
            f_codes = quantised.tile([P, HW], U32, name="f_codes", align_bytes=64)
            f_planes = quantised.tile([P, HW], U8, name="f_planes", align_bytes=64)
            for piece in range(HW // width):
                cols = slice(piece * width, (piece + 1) * width)
                nc.vector.quantize_mx(
                    out=f_codes[:, cols].bitcast(FP8X4),
                    scales=f_planes[:, cols],
                    in_=grouped[:, cols, :].rearrange("p x t -> p (x t)"),
                )
            return f_codes, f_planes

        def round_product(acc):
            rounded = []
            for i in range(HW_TILES):
                tile = stage.tile([P, O], BF16, name="rounded")
                copy = nc.scalar.copy if i % 2 == 0 else nc.vector.tensor_copy
                copy(
                    out=tile[:].rearrange("x (u p e) -> x u p e", u=PAIRS, e=PACK // PAIRS),
                    in_=acc[i][:].rearrange("x (p u e) -> x u p e", u=PAIRS, e=PACK // PAIRS),
                )
                rounded.append(tile)
            return rounded

        def turn_product(rounded):
            turned = []
            for i in range(HW_TILES):
                tile = psum.tile([P, PAIRS, P], F32, name="turned%d" % i, tag="bank%d" % i)
                pair_words = rounded[i][:].bitcast(F32)
                for u in range(PAIRS):
                    nc.tensor.transpose(tile[:, u, :], pair_words[:, u * P : (u + 1) * P], identity[:])
                turned.append(tile)
            return turned

        def regroup_product(turned):
            grouped = []
            for i in range(HW_TILES):
                tile = stage.tile([P, P, PACK], BF16, name="product", align_bytes=64)
                copy = nc.vector.tensor_copy if i == 1 else nc.scalar.copy
                copy(
                    out=tile[:].rearrange("p x t -> p (x t)").bitcast(F32),
                    in_=turned[i][:].rearrange("p u x -> p x u"),
                )
                grouped.append(tile)
            return grouped

        def quantise_product(side, grouped):
            for i in range(HW_TILES):
                cols = slice(i * P, (i + 1) * P)
                nc.vector.quantize_mx(
                    out=codes[side][:, cols].bitcast(FP8X4),
                    scales=planes[side][:, cols],
                    in_=grouped[i][:].rearrange("p x t -> p (x t)"),
                )

        last = len(steps) - 1
        batch_at = {}
        for number, side in enumerate(sides):
            g = 0
            for count in BATCHES[side]:
                batch_at[number * PASSES + g] = (side, g, count)
                g += count
        raws = load_batch(*batch_at[0])
        groupeds = {0: regroup_feature(raws[0], SHARES)}

        acc = {}
        for step, (side, g) in enumerate(steps):
            if step + 1 in batch_at:
                raws += load_batch(*batch_at[step + 1])
            if step + 1 <= last - AT_ONCE:
                groupeds[step + 1] = regroup_feature(raws[step + 1], SHARES)
            fine = step > last - FINE
            if step > last - AT_ONCE:
                groupeds[step] = regroup_feature(raws[step], [P] * HW_TILES if fine else SHARES_AT_ONCE)
            f_codes, f_planes = quantise_feature(groupeds[step], P if fine else HW)

            if g == 0:
                first = HW_TILES * sides.index(side)
                acc[side] = [
                    psum.tile([P, O], F32, name="acc%d" % (first + i), tag="bank%d" % (first + i))
                    for i in range(HW_TILES)
                ]
            block, j = divmod(g, SHARED)
            for i in range(HW_TILES):
                positions = slice(i * P, (i + 1) * P)
                nc.tensor.matmul_mx(
                    out=acc[side][i][:],
                    lhsT=f_codes[:, positions].bitcast(FP8X4),
                    lhsT_scale=f_planes[:, positions],
                    rhs=w_codes[side][:, g, :].bitcast(FP8X4),
                    rhs_scale=w_planes[side][4 * j : P, block, :],
                    start=(g == 0),
                    stop=(g == PASSES - 1),
                )

            if side == "k":
                if g == 0:
                    q_rounded = round_product(acc["q"])
                elif g == 1:
                    q_turned = turn_product(q_rounded)
                elif g == 2:
                    q_grouped = regroup_product(q_turned)
                elif g == 3:
                    quantise_product("q", q_grouped)

        k_rounded = round_product(acc["k"])
        k_turned = turn_product(k_rounded)
        k_grouped = regroup_product(k_turned)
        quantise_product("k", k_grouped)

        for i in range(HW_TILES):
            h, x_tile = divmod(i, W_TILES)
            x_cols = slice(i * P, (i + 1) * P)
            bank = "bank%d" % (HW_TILES + i)
            dots = psum.tile([P, W_TILES, P], F32, name="dots%d" % i, tag=bank)
            for w_tile in range(W_TILES):
                w_cols = slice(h * W + w_tile * P, h * W + (w_tile + 1) * P)
                nc.tensor.matmul_mx(
                    out=dots[:, w_tile, :],
                    lhsT=codes["q"][:, w_cols].bitcast(FP8X4),
                    lhsT_scale=planes["q"][:, w_cols],
                    rhs=codes["k"][:, x_cols].bitcast(FP8X4),
                    rhs_scale=planes["k"][:, x_cols],
                    start=True,
                    stop=True,
                )
            result = stage.tile([P, W_TILES, P], F32, name="result")
            if i % 2 == 0:
                nc.scalar.activation(out=result[:], in_=dots[:], func=COPY, scale=SCALE)
            else:
                nc.vector.tensor_scalar_mul(out=result[:], in0=dots[:], scalar1=SCALE)
            nc.sync.dma_start(
                out=out[0, h].rearrange("(i p) x -> p i x", p=P)[:, :, x_tile * P : (x_tile + 1) * P],
                in_=result[:],
            )
